import numpy as np
import ml_dtypes


def mxq(x, axis, fmt="e4m3"):
    dtype, down = {"e4m3": (ml_dtypes.float8_e4m3fn, 7), "e5m2": (ml_dtypes.float8_e5m2, 14)}[fmt]
    v = np.moveaxis(np.asarray(x, np.float32).astype(ml_dtypes.bfloat16).astype(np.float64), axis, -1)
    blocks = v.reshape(v.shape[:-1] + (-1, 32))
    amax = np.abs(blocks).max(-1, keepdims=True)
    byte = np.maximum(np.where(amax > 0, np.frexp(amax)[1] - 1 + 127, 0) - down, 1)
    scale = np.exp2(byte - 127.0)
    codes = (blocks / scale).astype(np.float32).astype(dtype).astype(np.float64)
    return np.moveaxis((codes * scale).reshape(v.shape), -1, axis)


WIDE = False


def mx_kscale(k):
    if not WIDE:
        return np.ones(k)
    levels = np.array([18, -18])
    if k % 512:
        return np.exp2(np.random.permutation(np.resize(levels, k // 32))).repeat(32)
    a = np.empty((k // 512, 16))
    for p in range(k // 512):
        a[p, :8] = np.random.permutation(np.resize(levels, 8))
        for g in range(8):
            far = levels[np.abs(levels - a[p, g]) >= 10]
            a[p, g + 8] = far[np.random.randint(len(far))]
    return np.exp2(a.ravel()).repeat(32)


BF16 = ml_dtypes.bfloat16


def bf(x):
    return np.asarray(x, np.float32).astype(BF16)


def f64(x):
    return np.asarray(x).astype(np.float64)


B, HALF, MID = 512, 512, 2048
D = 2 * HALF


def setup_inputs():
    s = mx_kscale(B)[:, None]
    u = mx_kscale(HALF)
    v = mx_kscale(MID)
    x = bf(np.random.standard_normal((B, D)))
    h3_0 = bf(np.maximum(np.random.standard_normal((B, MID)), 0.0))
    W4_0 = bf(np.random.standard_normal((MID, MID)) * np.sqrt(2.0 / MID))
    b4 = bf(np.random.standard_normal(MID) * 0.2)
    W5_0 = bf(np.random.standard_normal((MID, HALF)) * np.sqrt(2.0 / MID))
    b5 = bf(np.random.standard_normal(HALF) * 0.2)
    z4 = f64(h3_0) @ f64(W4_0) + f64(b4)
    for _ in range(100):
        bad = np.abs(z4).min(axis=1) < 1e-5
        if not bad.any():
            break
        h3_0[bad] = bf(np.maximum(np.random.standard_normal((int(bad.sum()), MID)), 0.0))
        z4[bad] = f64(h3_0[bad]) @ f64(W4_0) + f64(b4)
    g = bf(np.random.standard_normal((B, D)) * np.exp2(np.random.randint(-6, 1, (B, 1))) * 4.0 / s * np.repeat(u, 2))
    return {"x": x,
            "h3": bf(f64(h3_0) * s),
            "W4": bf(f64(W4_0) / v),
            "b4": b4,
            "W5": bf(f64(W5_0) * v[:, None] / u),
            "b5": b5,
            "z4": np.asarray(z4, np.float32),
            "grad_out": g}


def reference(x, h3, W4, b4, W5, b5, z4, grad_out):
    dm = f64(grad_out)[:, 0::2]
    dh = mxq(dm, 1, "e5m2") @ mxq(f64(W5), 1, "e4m3").T
    dz1 = dh * (f64(z4) > 0.0)
    dh3 = mxq(dz1, 1, "e5m2") @ mxq(f64(W4), 1, "e4m3").T
    dW4 = mxq(f64(h3), 0, "e4m3").T @ mxq(dz1, 0, "e5m2")
    return dh3, dW4

@@ -1,0 +1,287 @@
+from contextlib import ExitStack
+
+import concourse.mybir as mybir
+from concourse.masks import make_identity
+
+B, HALF, MID = 512, 512, 2048
+FLOPS = 2 * B * HALF * MID + 2 * (2 * B * MID * MID)
+BYTES = B * HALF * 2 + MID * HALF * 2 + B * MID * 4 + B * MID * 2 + MID * MID * 2 + B * MID * 4 + MID * MID * 4
+
+F32 = mybir.dt.float32
+BF16 = mybir.dt.bfloat16
+U32 = mybir.dt.uint32
+U8 = mybir.dt.uint8
+E4M3 = mybir.dt.float8_e4m3fn_x4
+E5M2 = mybir.dt.float8_e5m2_x4
+ALU = mybir.AluOpType
+
+P = 128
+N = 512
+Q = 4
+
+
+def tile_additivecoupling_pa_v_kernel(tc, x, h3, W4, b4, W5, b5, z4, grad_out, out_0, out_1):
+    nc = tc.nc
+    with ExitStack() as ctx:
+        const = ctx.enter_context(tc.tile_pool(name="const", bufs=1))
+        big = ctx.enter_context(tc.tile_pool(name="big", bufs=14))
+        wpool = ctx.enter_context(tc.tile_pool(name="wpool", bufs=4))
+        gpool = ctx.enter_context(tc.tile_pool(name="gpool", bufs=6))
+        psum = ctx.enter_context(tc.psum_pool(name="psum", bufs=4))
+        ctx.enter_context(tc.manual_schedule())
+
+        ident = const.tile([P, P], F32, name="ident")
+        make_identity(nc, ident[:])
+
+        dm_codes = const.tile([P, N], U32, name="dm_codes", align_bytes=64)
+        dm_scales = const.tile([P, N], U8, name="dm_scales", align_bytes=64)
+        h3_codes = const.tile([P, MID], U32, name="h3_codes", align_bytes=64)
+        h3_scales = const.tile([P, MID], U8, name="h3_scales", align_bytes=64)
+        tok_codes = const.tile([P, MID], U32, name="tok_codes", align_bytes=64)
+        tok_scales = const.tile([P, MID], U8, name="tok_scales", align_bytes=64)
+        feat_codes = const.tile([P, Q, Q, P], U32, name="feat_codes", align_bytes=64)
+        feat_scales = const.tile([P, Q, Q, P], U8, name="feat_scales", align_bytes=64)
+        dz = const.tile([P, Q, MID], BF16, name="dz", align_bytes=64)
+
+        def copy(engine, out, in_):
+            if engine == "S":
+                nc.scalar.copy(out=out, in_=in_)
+            else:
+                nc.vector.tensor_copy(out=out, in_=in_)
+
+        def big_tile(shape, dtype, name):
+            t = big.tile(shape, dtype, tag="big", name=name, align_bytes=64)
+            return t
+
+        def w_tiles(name):
+            c = wpool.tile([P, Q, N], U32, tag="wcodes", name=name + "_codes", align_bytes=64)
+            s = wpool.tile([P, Q, N], U8, tag="wscales", name=name + "_scales", align_bytes=64)
+            return c, s
+
+        def turn(rows, name):
+            banks = []
+            for half in range(2):
+                bank = psum.tile([P, 2, 2, P], F32, tag="tr", name=name + "_tr%d" % half)
+                for k in range(2):
+                    for u in range(2):
+                        nc.tensor.transpose(bank[:, k, u, :], rows[2 * half + k][:, u::2], ident[:])
+                banks.append(bank)
+            return banks
+
+        def gather(banks, engines, name):
+            g = gpool.tile([P, N, Q], BF16, tag="grouped", name=name + "_g", align_bytes=64)
+            words = g[:].rearrange("p c t -> p (c t)").bitcast(F32)
+            for half in range(2):
+                dst = words[:, 512 * half : 512 * (half + 1)].rearrange("p (k r u) -> p k r u", k=2, u=2)
+                copy(engines[half], dst, banks[half][:].rearrange("p k u r -> p k r u"))
+            return g
+
+        def quantize(g, codes, scales, fmt):
+            nc.vector.quantize_mx(out=codes.bitcast(fmt), scales=scales, in_=g[:].rearrange("p c t -> p (c t)"))
+
+        raw_g = big_tile([P, Q, 2 * HALF], BF16, "raw_g")
+        nc.sync.dma_start(out=raw_g[:], in_=grad_out.rearrange("(p j) d -> p j d", j=Q))
+        raw_w5 = []
+        for h in range(2):
+            t = big_tile([P, 2, Q, HALF], BF16, "raw_w5_%d" % h)
+            nc.sync.dma_start(out=t[:], in_=W5[1024 * h : 1024 * (h + 1), :].rearrange("(a p j) k -> p a j k", a=2, j=Q))
+            raw_w5.append(t)
+        z4_view = z4.rearrange("(p j) o -> p j o", j=Q)
+        raw_z4 = []
+        raw_w4 = {}
+        raw_h3 = []
+        h3_view = h3.rearrange("(p j) i -> p j i", j=Q)
+
+        def load_z4(t):
+            zt = big_tile([P, MID], F32, "raw_z4_%d" % t)
+            nc.sync.dma_start(out=zt[:], in_=z4_view[:, t, :])
+            raw_z4.append(zt)
+
+        def load_h3(h):
+            t = big_tile([P, Q, 1024], BF16, "raw_h3_%d" % h)
+            nc.sync.dma_start(out=t[:], in_=h3_view[:, :, 1024 * h : 1024 * (h + 1)])
+            raw_h3.append(t)
+
+        def load_w4(i):
+            q, h = divmod(i, 2)
+            view = W4[N * q : N * (q + 1), :].rearrange("(p j) o -> p j o", j=Q)
+            t = big_tile([P, 2, MID], BF16, "raw_w4_%d_%d" % (q, h))
+            nc.sync.dma_start(out=t[:], in_=view[:, 2 * h : 2 * h + 2, :])
+            raw_w4[q, h] = t
+
+        loads = {"z": load_z4, "h": load_h3, "w": load_w4}
+        order = "h0 z0 z1 z2 z3 w0 w1 h1 w2 w3 w4 w5 w6 w7".split()
+        for name in order[:11]:
+            loads[name[0]](int(name[1]))
+
+        even = gpool.tile([P, Q, HALF], BF16, tag="grouped", name="even", align_bytes=64)
+        evens = raw_g[:].rearrange("p j (k two) -> p j k two", two=2)[:, :, :, 0]
+        nc.vector.tensor_copy(out=even[:, 0:2, :], in_=evens[:, 0:2, :])
+        nc.scalar.copy(out=even[:, 2:4, :], in_=evens[:, 2:4, :])
+        banks = turn([even[:, j, :].bitcast(F32) for j in range(Q)], "dm")
+        g = gather(banks, "VS", "dm")
+        quantize(g, dm_codes[:], dm_scales[:], E5M2)
+
+        w5_codes, w5_scales = w_tiles("w5")
+        w5_g = []
+        for a in range(Q):
+            banks = turn([raw_w5[a // 2][:, a % 2, j, :].bitcast(F32) for j in range(Q)], "w5_%d" % a)
+            g = gather(banks, ("SS", "VV", "SS", "SS")[a], "w5_%d" % a)
+            w5_g.append(g)
+            if a >= 1:
+                quantize(w5_g[a - 1], w5_codes[:, a - 1, :], w5_scales[:, a - 1, :], E4M3)
+        quantize(w5_g[3], w5_codes[:, 3, :], w5_scales[:, 3, :], E4M3)
+        for name in order[11:]:
+            loads[name[0]](int(name[1]))
+
+        def make_dz(t):
+            for a in range(Q):
+                acc = psum.tile([P, N], F32, tag="mm", name="dh_%d_%d" % (t, a))
+                nc.tensor.matmul_mx(
+                    out=acc[:],
+                    lhsT=dm_codes[:, P * t : P * (t + 1)].bitcast(E5M2),
+                    lhsT_scale=dm_scales[:, P * t : P * (t + 1)],
+                    rhs=w5_codes[:, a, :].bitcast(E4M3),
+                    rhs_scale=w5_scales[:, a, :],
+                    start=True,
+                    stop=True,
+                )
+                cols = slice(N * a, N * (a + 1))
+                nc.vector.scalar_tensor_tensor(
+                    out=dz[:, t, cols].rearrange("p (m j) -> p m j", j=Q),
+                    in0=raw_z4[t][:, cols].rearrange("p (m j) -> p m j", j=Q),
+                    scalar=0.0,
+                    in1=acc[:].rearrange("p (j m) -> p m j", j=Q),
+                    op0=ALU.is_gt,
+                    op1=ALU.mult,
+                )
+
+        def turn_dz(t):
+            banks = turn([dz[:, t, N * g : N * (g + 1)].bitcast(F32) for g in range(Q)], "dz_%d" % t)
+            return gather(banks, "SS", "dz_%d" % t)
+
+        def quant_dz(t, g):
+            quantize(
+                g,
+                feat_codes[:, t, :, :].rearrange("p g r -> p (g r)"),
+                feat_scales[:, t, :, :].rearrange("p g r -> p (g r)"),
+                E5M2,
+            )
+
+        def interleave(engine, src, name):
+            g = gpool.tile([P, N, Q], BF16, tag="grouped", name=name + "_g", align_bytes=64)
+            copy(
+                engine,
+                g[:].rearrange("p (c i) t -> p c t i", i=4),
+                src.rearrange("p t (c i) -> p c t i", i=4),
+            )
+            return g
+
+        def tok_il(engine, a):
+            return interleave(engine, dz[:, :, N * a : N * (a + 1)], "tok_%d" % a)
+
+        def tok_q(a, g):
+            quantize(g, tok_codes[:, N * a : N * (a + 1)], tok_scales[:, N * a : N * (a + 1)], E5M2)
+
+        def h3_il(engine, a):
+            return interleave(engine, raw_h3[a // 2][:, :, N * (a % 2) : N * (a % 2 + 1)], "h3_%d" % a)
+
+        def h3_q(a, g):
+            quantize(g, h3_codes[:, N * a : N * (a + 1)], h3_scales[:, N * a : N * (a + 1)], E4M3)
+
+        w4_codes = {}
+
+        def turn_w4(m, engines):
+            q, g = divmod(m, Q)
+            if g == 0:
+                w4_codes[q] = w_tiles("w4_%d" % q)
+            banks = turn(
+                [raw_w4[q, j // 2][:, j % 2, N * g : N * (g + 1)].bitcast(F32) for j in range(Q)], "w4_%d" % m
+            )
+            return gather(banks, engines, "w4_%d" % m)
+
+        def quant_w4(m, gt):
+            q, g = divmod(m, Q)
+            quantize(gt, w4_codes[q][0][:, g, :], w4_codes[q][1][:, g, :], E4M3)
+
+        h0 = h3_il("S", 0)
+        make_dz(0)
+        h3_q(0, h0)
+        make_dz(1)
+        f0 = turn_dz(0)
+        h1 = h3_il("S", 1)
+        make_dz(2)
+        quant_dz(0, f0)
+        f1 = turn_dz(1)
+        make_dz(3)
+        f2 = turn_dz(2)
+        t0 = tok_il("V", 0)
+        t3 = tok_il("S", 3)
+        tok_q(0, t0)
+        quant_dz(1, f1)
+        t1 = tok_il("V", 1)
+        f3 = turn_dz(3)
+        tok_q(1, t1)
+        t2 = tok_il("V", 2)
+        u0 = turn_w4(0, "SS")
+        tok_q(2, t2)
+        tok_q(3, t3)
+        quant_dz(2, f2)
+        quant_dz(3, f3)
+        u1 = turn_w4(1, "SS")
+
+        def out1_tile(s, engines):
+            stage = big_tile([P, MID], F32, "stage1_%d" % s)
+            rows = slice(P * s, P * (s + 1))
+            for a in range(Q):
+                cols = slice(N * a, N * (a + 1))
+                acc = psum.tile([P, N], F32, tag="mm", name="o1_%d_%d" % (s, a))
+                nc.tensor.matmul_mx(
+                    out=acc[:],
+                    lhsT=h3_codes[:, rows].bitcast(E4M3),
+                    lhsT_scale=h3_scales[:, rows],
+                    rhs=tok_codes[:, cols].bitcast(E5M2),
+                    rhs_scale=tok_scales[:, cols],
+                    start=True,
+                    stop=True,
+                )
+                copy(engines[a], stage[:, cols], acc[:])
+            nc.sync.dma_start(out=out_1[rows, :], in_=stage[:])
+
+        pending = [(0, u0), (1, u1)]
+        h3_q(1, h1)
+        h3_at = {4: 2, 7: 3}
+        for n in range(16):
+            gt = turn_w4(n + 2, "SS") if n < 14 else None
+            out1_tile(n, "SVSV")
+            if pending:
+                quant_w4(*pending.pop(0))
+            if gt is not None:
+                pending.append((n + 2, gt))
+            if n in h3_at:
+                a = h3_at[n]
+                hg = h3_il("V", a)
+                h3_q(a, hg)
+
+        out0_view = out_0.rearrange("(p j) i -> p j i", j=Q)
+        for t in range(Q):
+            stage = big_tile([P, MID], F32, "stage0_%d" % t)
+            for q in range(Q):
+                codes, scales = w4_codes[q]
+                acc = psum.tile([P, N], F32, tag="mm", name="o0_%d_%d" % (q, t))
+                for g in range(Q):
+                    nc.tensor.matmul_mx(
+                        out=acc[:],
+                        lhsT=feat_codes[:, t, g, :].bitcast(E5M2),
+                        lhsT_scale=feat_scales[:, t, g, :],
+                        rhs=codes[:, g, :].bitcast(E4M3),
+                        rhs_scale=scales[:, g, :],
+                        start=(g == 0),
+                        stop=(g == Q - 1),
+                    )
+                copy(
+                    "SV"[q % 2],
+                    stage[:, N * q : N * (q + 1)].rearrange("p (m j) -> p m j", j=Q),
+                    acc[:].rearrange("p (j m) -> p m j", j=Q),
+                )
+            nc.sync.dma_start(out=out0_view[:, t, :], in_=stage[:])

@@ -5,7 +5,7 @@ from concourse.masks import make_identity
 
 B, HALF, MID = 512, 512, 2048
 FLOPS = 2 * B * HALF * MID + 2 * (2 * B * MID * MID)
-BYTES = B * HALF * 2 + MID * HALF * 2 + B * MID * 4 + B * MID * 2 + MID * MID * 2 + B * MID * 4 + MID * MID * 4
+BYTES = 2 * B * HALF + 2 * MID * HALF + 4 * B * MID + 2 * B * MID + 2 * MID * MID + 4 * B * MID + 4 * MID * MID
 
 F32 = mybir.dt.float32
 BF16 = mybir.dt.bfloat16
@@ -16,32 +16,32 @@ E5M2 = mybir.dt.float8_e5m2_x4
 ALU = mybir.AluOpType
 
 P = 128
+J = 4
 N = 512
-Q = 4
+STEPS = 16
+LATE_FEATURES = 5
 
 
 def tile_additivecoupling_pa_v_kernel(tc, x, h3, W4, b4, W5, b5, z4, grad_out, out_0, out_1):
     nc = tc.nc
     with ExitStack() as ctx:
         const = ctx.enter_context(tc.tile_pool(name="const", bufs=1))
-        big = ctx.enter_context(tc.tile_pool(name="big", bufs=14))
-        wpool = ctx.enter_context(tc.tile_pool(name="wpool", bufs=4))
-        gpool = ctx.enter_context(tc.tile_pool(name="gpool", bufs=6))
+        big = ctx.enter_context(tc.tile_pool(name="big", bufs=15))
+        wide = ctx.enter_context(tc.tile_pool(name="wide", bufs=4))
+        small = ctx.enter_context(tc.tile_pool(name="small", bufs=9))
         psum = ctx.enter_context(tc.psum_pool(name="psum", bufs=4))
         ctx.enter_context(tc.manual_schedule())
 
         ident = const.tile([P, P], F32, name="ident")
         make_identity(nc, ident[:])
-
-        dm_codes = const.tile([P, N], U32, name="dm_codes", align_bytes=64)
-        dm_scales = const.tile([P, N], U8, name="dm_scales", align_bytes=64)
+        dz2_codes = const.tile([P, N], U32, name="dz2_codes", align_bytes=64)
+        dz2_scales = const.tile([P, N], U8, name="dz2_scales", align_bytes=64)
         h3_codes = const.tile([P, MID], U32, name="h3_codes", align_bytes=64)
         h3_scales = const.tile([P, MID], U8, name="h3_scales", align_bytes=64)
         tok_codes = const.tile([P, MID], U32, name="tok_codes", align_bytes=64)
         tok_scales = const.tile([P, MID], U8, name="tok_scales", align_bytes=64)
-        feat_codes = const.tile([P, Q, Q, P], U32, name="feat_codes", align_bytes=64)
-        feat_scales = const.tile([P, Q, Q, P], U8, name="feat_scales", align_bytes=64)
-        dz = const.tile([P, Q, MID], BF16, name="dz", align_bytes=64)
+        feat_codes = const.tile([P, J, 4, P], U32, name="feat_codes", align_bytes=64)
+        feat_scales = const.tile([P, J, 4, P], U8, name="feat_scales", align_bytes=64)
 
         def copy(engine, out, in_):
             if engine == "S":
@@ -49,193 +49,188 @@ def tile_additivecoupling_pa_v_kernel(tc, x, h3, W4, b4, W5, b5, z4, grad_out, o
             else:
                 nc.vector.tensor_copy(out=out, in_=in_)
 
-        def big_tile(shape, dtype, name):
-            t = big.tile(shape, dtype, tag="big", name=name, align_bytes=64)
-            return t
+        def load(shape, dtype, name, source):
+            raw = big.tile(shape, dtype, tag="big", name=name, align_bytes=64)
+            nc.sync.dma_start(out=raw[:], in_=source)
+            return raw
 
-        def w_tiles(name):
-            c = wpool.tile([P, Q, N], U32, tag="wcodes", name=name + "_codes", align_bytes=64)
-            s = wpool.tile([P, Q, N], U8, tag="wscales", name=name + "_scales", align_bytes=64)
-            return c, s
+        def quantize(grouped, codes, scales, fmt):
+            nc.vector.quantize_mx(out=codes.bitcast(fmt), scales=scales, in_=grouped[:].rearrange("p c t -> p (c t)"))
 
-        def turn(rows, name):
+        def turn(rows, engines, name):
             banks = []
-            for half in range(2):
-                bank = psum.tile([P, 2, 2, P], F32, tag="tr", name=name + "_tr%d" % half)
-                for k in range(2):
+            for pair in range(2):
+                bank = psum.tile([P, 2, 2, P], F32, tag="turned", name="%s_bank_%d" % (name, pair))
+                for i in range(2):
+                    words = rows[2 * pair + i].bitcast(F32)
                     for u in range(2):
-                        nc.tensor.transpose(bank[:, k, u, :], rows[2 * half + k][:, u::2], ident[:])
+                        nc.tensor.transpose(bank[:, i, u, :], words[:, u::2], ident[:])
                 banks.append(bank)
-            return banks
+            grouped = small.tile([P, N, J], BF16, tag="grouped", name=name, align_bytes=64)
+            out_words = grouped[:].rearrange("p c t -> p (c t)").bitcast(F32)
+            for pair in range(2):
+                half = out_words[:, N * pair : N * (pair + 1)].rearrange("p (i r u) -> p i r u", i=2, u=2)
+                copy(engines[pair], half, banks[pair][:].rearrange("p i u r -> p i r u"))
+            return grouped
 
-        def gather(banks, engines, name):
-            g = gpool.tile([P, N, Q], BF16, tag="grouped", name=name + "_g", align_bytes=64)
-            words = g[:].rearrange("p c t -> p (c t)").bitcast(F32)
-            for half in range(2):
-                dst = words[:, 512 * half : 512 * (half + 1)].rearrange("p (k r u) -> p k r u", k=2, u=2)
-                copy(engines[half], dst, banks[half][:].rearrange("p k u r -> p k r u"))
-            return g
+        def interleave(engine, rows, name):
+            grouped = small.tile([P, N, J], BF16, tag="grouped", name=name, align_bytes=64)
+            copy(
+                engine,
+                grouped[:].rearrange("p (c i) t -> p c t i", i=4),
+                rows.rearrange("p t (c i) -> p c t i", i=4),
+            )
+            return grouped
 
-        def quantize(g, codes, scales, fmt):
-            nc.vector.quantize_mx(out=codes.bitcast(fmt), scales=scales, in_=g[:].rearrange("p c t -> p (c t)"))
+        z4_rows = z4.rearrange("(p j) o -> p j o", j=J)
+        h3_rows = h3.rearrange("(p j) i -> p j i", j=J)
+        raw_w5, raw_z4, raw_h3, raw_w4 = {}, {}, {}, {}
 
-        raw_g = big_tile([P, Q, 2 * HALF], BF16, "raw_g")
-        nc.sync.dma_start(out=raw_g[:], in_=grad_out.rearrange("(p j) d -> p j d", j=Q))
-        raw_w5 = []
-        for h in range(2):
-            t = big_tile([P, 2, Q, HALF], BF16, "raw_w5_%d" % h)
-            nc.sync.dma_start(out=t[:], in_=W5[1024 * h : 1024 * (h + 1), :].rearrange("(a p j) k -> p a j k", a=2, j=Q))
-            raw_w5.append(t)
-        z4_view = z4.rearrange("(p j) o -> p j o", j=Q)
-        raw_z4 = []
-        raw_w4 = {}
-        raw_h3 = []
-        h3_view = h3.rearrange("(p j) i -> p j i", j=Q)
+        def load_w5(half):
+            rows = W5[2 * N * half : 2 * N * (half + 1), :].rearrange("(a p j) k -> p a j k", a=2, j=J)
+            raw_w5[half] = load([P, 2, J, HALF], BF16, "raw_w5_%d" % half, rows)
 
         def load_z4(t):
-            zt = big_tile([P, MID], F32, "raw_z4_%d" % t)
-            nc.sync.dma_start(out=zt[:], in_=z4_view[:, t, :])
-            raw_z4.append(zt)
+            raw_z4[t] = load([P, MID], F32, "raw_z4_%d" % t, z4_rows[:, t, :])
 
-        def load_h3(h):
-            t = big_tile([P, Q, 1024], BF16, "raw_h3_%d" % h)
-            nc.sync.dma_start(out=t[:], in_=h3_view[:, :, 1024 * h : 1024 * (h + 1)])
-            raw_h3.append(t)
+        def load_h3(half):
+            cols = slice(2 * N * half, 2 * N * (half + 1))
+            raw_h3[half] = load([P, J, 2 * N], BF16, "raw_h3_%d" % half, h3_rows[:, :, cols])
 
-        def load_w4(i):
-            q, h = divmod(i, 2)
-            view = W4[N * q : N * (q + 1), :].rearrange("(p j) o -> p j o", j=Q)
-            t = big_tile([P, 2, MID], BF16, "raw_w4_%d_%d" % (q, h))
-            nc.sync.dma_start(out=t[:], in_=view[:, 2 * h : 2 * h + 2, :])
-            raw_w4[q, h] = t
+        def load_w4(q, half):
+            rows = W4[N * q : N * (q + 1), :].rearrange("(p j) o -> p j o", j=J)
+            raw_w4[q, half] = load([P, 2, MID], BF16, "raw_w4_%d_%d" % (q, half), rows[:, 2 * half : 2 * half + 2, :])
 
-        loads = {"z": load_z4, "h": load_h3, "w": load_w4}
-        order = "h0 z0 z1 z2 z3 w0 w1 h1 w2 w3 w4 w5 w6 w7".split()
-        for name in order[:11]:
-            loads[name[0]](int(name[1]))
+        raw_grad = load([P, J, 2 * HALF], BF16, "raw_grad", grad_out.rearrange("(p j) d -> p j d", j=J))
+        load_w5(0)
+        load_w5(1)
+        load_z4(0)
+        load_z4(1)
+        load_h3(0)
+        load_z4(2)
+        load_z4(3)
+        load_w4(0, 0)
+        load_w4(0, 1)
+        load_h3(1)
+        load_w4(1, 0)
 
-        even = gpool.tile([P, Q, HALF], BF16, tag="grouped", name="even", align_bytes=64)
-        evens = raw_g[:].rearrange("p j (k two) -> p j k two", two=2)[:, :, :, 0]
-        nc.vector.tensor_copy(out=even[:, 0:2, :], in_=evens[:, 0:2, :])
-        nc.scalar.copy(out=even[:, 2:4, :], in_=evens[:, 2:4, :])
-        banks = turn([even[:, j, :].bitcast(F32) for j in range(Q)], "dm")
-        g = gather(banks, "VS", "dm")
-        quantize(g, dm_codes[:], dm_scales[:], E5M2)
+        w5_codes = wide.tile([P, 4, N], U32, tag="wide", name="w5_codes", align_bytes=64)
+        w5_scales = wide.tile([P, 4, N], U8, tag="scales", name="w5_scales", align_bytes=64)
 
-        w5_codes, w5_scales = w_tiles("w5")
-        w5_g = []
-        for a in range(Q):
-            banks = turn([raw_w5[a // 2][:, a % 2, j, :].bitcast(F32) for j in range(Q)], "w5_%d" % a)
-            g = gather(banks, ("SS", "VV", "SS", "SS")[a], "w5_%d" % a)
-            w5_g.append(g)
-            if a >= 1:
-                quantize(w5_g[a - 1], w5_codes[:, a - 1, :], w5_scales[:, a - 1, :], E4M3)
-        quantize(w5_g[3], w5_codes[:, 3, :], w5_scales[:, 3, :], E4M3)
-        for name in order[11:]:
-            loads[name[0]](int(name[1]))
+        even = small.tile([P, J, HALF], BF16, tag="grouped", name="even", align_bytes=64)
+        even_cols = raw_grad[:].rearrange("p j (k two) -> p j k two", two=2)[:, :, :, 0]
+        nc.vector.tensor_copy(out=even[:, 0:2, :], in_=even_cols[:, 0:2, :])
+        nc.scalar.copy(out=even[:, 2:J, :], in_=even_cols[:, 2:J, :])
+        dz2_grouped = turn([even[:, j, :] for j in range(J)], "SS", "dz2_grouped")
+        quantize(dz2_grouped, dz2_codes[:], dz2_scales[:], E5M2)
 
-        def make_dz(t):
-            for a in range(Q):
-                acc = psum.tile([P, N], F32, tag="mm", name="dh_%d_%d" % (t, a))
+        def turn_w5(a):
+            return turn([raw_w5[a // 2][:, a % 2, j, :] for j in range(J)], "SS", "w5_grouped_%d" % a)
+
+        def quantize_w5(a, grouped):
+            quantize(grouped, w5_codes[:, a, :], w5_scales[:, a, :], E4M3)
+
+        w5_grouped = turn_w5(0)
+        for a in range(1, 4):
+            w5_next = turn_w5(a)
+            quantize_w5(a - 1, w5_grouped)
+            w5_grouped = w5_next
+        quantize_w5(3, w5_grouped)
+
+        dz1 = []
+        for half in range(2):
+            dz1_half = wide.tile([P, J, 2 * N], BF16, tag="wide", name="dz1_%d" % half, align_bytes=64)
+            dz1.append(dz1_half)
+
+        def dz1_chunk(a):
+            return dz1[a // 2][:, :, N * (a % 2) : N * (a % 2 + 1)]
+
+        def make_dz1(t):
+            for a in range(4):
+                dh = psum.tile([P, N], F32, tag="sums", name="dh_%d_%d" % (t, a))
                 nc.tensor.matmul_mx(
-                    out=acc[:],
-                    lhsT=dm_codes[:, P * t : P * (t + 1)].bitcast(E5M2),
-                    lhsT_scale=dm_scales[:, P * t : P * (t + 1)],
+                    out=dh[:],
+                    lhsT=dz2_codes[:, P * t : P * (t + 1)].bitcast(E5M2),
+                    lhsT_scale=dz2_scales[:, P * t : P * (t + 1)],
                     rhs=w5_codes[:, a, :].bitcast(E4M3),
                     rhs_scale=w5_scales[:, a, :],
                     start=True,
                     stop=True,
                 )
-                cols = slice(N * a, N * (a + 1))
                 nc.vector.scalar_tensor_tensor(
-                    out=dz[:, t, cols].rearrange("p (m j) -> p m j", j=Q),
-                    in0=raw_z4[t][:, cols].rearrange("p (m j) -> p m j", j=Q),
+                    out=dz1_chunk(a)[:, t, :].rearrange("p (m j) -> p m j", j=J),
+                    in0=raw_z4[t][:, N * a : N * (a + 1)].rearrange("p (m j) -> p m j", j=J),
                     scalar=0.0,
-                    in1=acc[:].rearrange("p (j m) -> p m j", j=Q),
+                    in1=dh[:].rearrange("p (j m) -> p m j", j=J),
                     op0=ALU.is_gt,
                     op1=ALU.mult,
                 )
 
-        def turn_dz(t):
-            banks = turn([dz[:, t, N * g : N * (g + 1)].bitcast(F32) for g in range(Q)], "dz_%d" % t)
-            return gather(banks, "SS", "dz_%d" % t)
+        def turn_dz1(t):
+            return turn([dz1_chunk(g)[:, t, :] for g in range(4)], "SS", "feat_grouped_%d" % t)
 
-        def quant_dz(t, g):
-            quantize(
-                g,
-                feat_codes[:, t, :, :].rearrange("p g r -> p (g r)"),
-                feat_scales[:, t, :, :].rearrange("p g r -> p (g r)"),
-                E5M2,
-            )
+        def quantize_feat(t, grouped):
+            codes = feat_codes[:, t, :, :].rearrange("p g r -> p (g r)")
+            scales = feat_scales[:, t, :, :].rearrange("p g r -> p (g r)")
+            quantize(grouped, codes, scales, E5M2)
 
-        def interleave(engine, src, name):
-            g = gpool.tile([P, N, Q], BF16, tag="grouped", name=name + "_g", align_bytes=64)
-            copy(
-                engine,
-                g[:].rearrange("p (c i) t -> p c t i", i=4),
-                src.rearrange("p t (c i) -> p c t i", i=4),
-            )
-            return g
+        def interleave_tok(engine, a):
+            return interleave(engine, dz1_chunk(a), "tok_grouped_%d" % a)
 
-        def tok_il(engine, a):
-            return interleave(engine, dz[:, :, N * a : N * (a + 1)], "tok_%d" % a)
+        def quantize_tok(a, grouped):
+            cols = slice(N * a, N * (a + 1))
+            quantize(grouped, tok_codes[:, cols], tok_scales[:, cols], E5M2)
 
-        def tok_q(a, g):
-            quantize(g, tok_codes[:, N * a : N * (a + 1)], tok_scales[:, N * a : N * (a + 1)], E5M2)
+        def interleave_h3(engine, a):
+            return interleave(engine, raw_h3[a // 2][:, :, N * (a % 2) : N * (a % 2 + 1)], "h3_grouped_%d" % a)
 
-        def h3_il(engine, a):
-            return interleave(engine, raw_h3[a // 2][:, :, N * (a % 2) : N * (a % 2 + 1)], "h3_%d" % a)
+        def quantize_h3(a, grouped):
+            cols = slice(N * a, N * (a + 1))
+            quantize(grouped, h3_codes[:, cols], h3_scales[:, cols], E4M3)
 
-        def h3_q(a, g):
-            quantize(g, h3_codes[:, N * a : N * (a + 1)], h3_scales[:, N * a : N * (a + 1)], E4M3)
+        feat_grouped = {}
+        make_dz1(0)
+        make_dz1(1)
+        load_w4(1, 1)
+        h3_grouped = interleave_h3("S", 0)
+        feat_grouped[0] = turn_dz1(0)
+        make_dz1(2)
+        feat_grouped[1] = turn_dz1(1)
+        make_dz1(3)
+        tok_grouped = {0: interleave_tok("S", 0)}
+        load_w4(2, 0)
+        load_w4(2, 1)
+        quantize_h3(0, h3_grouped)
+        feat_grouped[2] = turn_dz1(2)
+        tok_grouped[1] = interleave_tok("V", 1)
+        quantize_tok(0, tok_grouped[0])
+        tok_grouped[3] = interleave_tok("S", 3)
+        tok_grouped[2] = interleave_tok("V", 2)
+        quantize_tok(1, tok_grouped[1])
+        quantize_tok(2, tok_grouped[2])
+        feat_grouped[3] = turn_dz1(3)
+        quantize_tok(3, tok_grouped[3])
 
-        w4_codes = {}
+        w4_codes, w4_scales = {}, {}
 
-        def turn_w4(m, engines):
-            q, g = divmod(m, Q)
+        def turn_w4(unit):
+            q, g = divmod(unit, 4)
             if g == 0:
-                w4_codes[q] = w_tiles("w4_%d" % q)
-            banks = turn(
-                [raw_w4[q, j // 2][:, j % 2, N * g : N * (g + 1)].bitcast(F32) for j in range(Q)], "w4_%d" % m
-            )
-            return gather(banks, engines, "w4_%d" % m)
+                w4_codes[q] = wide.tile([P, 4, N], U32, tag="wide", name="w4_codes_%d" % q, align_bytes=64)
+                w4_scales[q] = wide.tile([P, 4, N], U8, tag="scales", name="w4_scales_%d" % q, align_bytes=64)
+            rows = [raw_w4[q, j // 2][:, j % 2, N * g : N * (g + 1)] for j in range(J)]
+            return turn(rows, "SS", "w4_grouped_%d" % unit)
 
-        def quant_w4(m, gt):
-            q, g = divmod(m, Q)
-            quantize(gt, w4_codes[q][0][:, g, :], w4_codes[q][1][:, g, :], E4M3)
+        def quantize_w4(unit, grouped):
+            q, g = divmod(unit, 4)
+            quantize(grouped, w4_codes[q][:, g, :], w4_scales[q][:, g, :], E4M3)
 
-        h0 = h3_il("S", 0)
-        make_dz(0)
-        h3_q(0, h0)
-        make_dz(1)
-        f0 = turn_dz(0)
-        h1 = h3_il("S", 1)
-        make_dz(2)
-        quant_dz(0, f0)
-        f1 = turn_dz(1)
-        make_dz(3)
-        f2 = turn_dz(2)
-        t0 = tok_il("V", 0)
-        t3 = tok_il("S", 3)
-        tok_q(0, t0)
-        quant_dz(1, f1)
-        t1 = tok_il("V", 1)
-        f3 = turn_dz(3)
-        tok_q(1, t1)
-        t2 = tok_il("V", 2)
-        u0 = turn_w4(0, "SS")
-        tok_q(2, t2)
-        tok_q(3, t3)
-        quant_dz(2, f2)
-        quant_dz(3, f3)
-        u1 = turn_w4(1, "SS")
-
-        def out1_tile(s, engines):
-            stage = big_tile([P, MID], F32, "stage1_%d" % s)
+        def out_1_tile(s):
             rows = slice(P * s, P * (s + 1))
-            for a in range(Q):
+            result = big.tile([P, MID], F32, tag="big", name="out_1_rows_%d" % s, align_bytes=64)
+            for a in range(4):
                 cols = slice(N * a, N * (a + 1))
-                acc = psum.tile([P, N], F32, tag="mm", name="o1_%d_%d" % (s, a))
+                acc = psum.tile([P, N], F32, tag="sums", name="out_1_%d_%d" % (s, a))
                 nc.tensor.matmul_mx(
                     out=acc[:],
                     lhsT=h3_codes[:, rows].bitcast(E4M3),
@@ -245,43 +240,46 @@ def tile_additivecoupling_pa_v_kernel(tc, x, h3, W4, b4, W5, b5, z4, grad_out, o
                     start=True,
                     stop=True,
                 )
-                copy(engines[a], stage[:, cols], acc[:])
-            nc.sync.dma_start(out=out_1[rows, :], in_=stage[:])
+                copy("VS"[a % 2], result[:, cols], acc[:])
+            nc.sync.dma_start(out=out_1[rows, :], in_=result[:])
 
-        pending = [(0, u0), (1, u1)]
-        h3_q(1, h1)
-        h3_at = {4: 2, 7: 3}
-        for n in range(16):
-            gt = turn_w4(n + 2, "SS") if n < 14 else None
-            out1_tile(n, "SVSV")
-            if pending:
-                quant_w4(*pending.pop(0))
-            if gt is not None:
-                pending.append((n + 2, gt))
-            if n in h3_at:
-                a = h3_at[n]
-                hg = h3_il("V", a)
-                h3_q(a, hg)
+        for s in range(STEPS):
+            w4_next = turn_w4(s)
+            chunk = s // 4 + 1
+            h3_due = s % 4 == 1 and chunk < 4
+            if h3_due:
+                h3_grouped = interleave_h3("V", chunk)
+            if s > 0:
+                quantize_w4(s - 1, w4_grouped)
+            w4_grouped = w4_next
+            if LATE_FEATURES <= s < LATE_FEATURES + J:
+                quantize_feat(s - LATE_FEATURES, feat_grouped[s - LATE_FEATURES])
+            out_1_tile(s)
+            if s < 2:
+                load_w4(3, s)
+            if h3_due:
+                quantize_h3(chunk, h3_grouped)
+        quantize_w4(STEPS - 1, w4_grouped)
 
-        out0_view = out_0.rearrange("(p j) i -> p j i", j=Q)
-        for t in range(Q):
-            stage = big_tile([P, MID], F32, "stage0_%d" % t)
-            for q in range(Q):
-                codes, scales = w4_codes[q]
-                acc = psum.tile([P, N], F32, tag="mm", name="o0_%d_%d" % (q, t))
-                for g in range(Q):
+        out_0_rows = out_0.rearrange("(p j) i -> p j i", j=J)
+        for t in range(J):
+            result = big.tile([P, MID], F32, tag="big", name="out_0_rows_%d" % t, align_bytes=64)
+            for q in range(4):
+                acc = psum.tile([P, N], F32, tag="sums", name="out_0_%d_%d" % (t, q))
+                for g in range(4):
                     nc.tensor.matmul_mx(
                         out=acc[:],
                         lhsT=feat_codes[:, t, g, :].bitcast(E5M2),
                         lhsT_scale=feat_scales[:, t, g, :],
-                        rhs=codes[:, g, :].bitcast(E4M3),
-                        rhs_scale=scales[:, g, :],
+                        rhs=w4_codes[q][:, g, :].bitcast(E4M3),
+                        rhs_scale=w4_scales[q][:, g, :],
                         start=(g == 0),
-                        stop=(g == Q - 1),
+                        stop=(g == 3),
                     )
-                copy(
-                    "SV"[q % 2],
-                    stage[:, N * q : N * (q + 1)].rearrange("p (m j) -> p m j", j=Q),
-                    acc[:].rearrange("p (j m) -> p m j", j=Q),
-                )
-            nc.sync.dma_start(out=out0_view[:, t, :], in_=stage[:])
+                cols = slice(N * q, N * (q + 1))
+                copy("SV"[q % 2], result[:, cols].rearrange("p (m j) -> p m j", j=J), acc[:].rearrange("p (j m) -> p m j", j=J))
+                if t == J - 1 and q >= 1:
+                    ready = slice(0 if q == 1 else N * q, N * (q + 1))
+                    nc.sync.dma_start(out=out_0_rows[:, t, ready], in_=result[:, ready])
+            if t < J - 1:
+                nc.sync.dma_start(out=out_0_rows[:, t, :], in_=result[:])

from contextlib import ExitStack

import concourse.mybir as mybir
from concourse.masks import make_identity

B, HALF, MID = 512, 512, 2048
FLOPS = 2 * B * HALF * MID + 2 * (2 * B * MID * MID)
BYTES = 2 * B * HALF + 2 * MID * HALF + 4 * B * MID + 2 * B * MID + 2 * MID * MID + 4 * B * MID + 4 * MID * MID

F32 = mybir.dt.float32
BF16 = mybir.dt.bfloat16
U32 = mybir.dt.uint32
U8 = mybir.dt.uint8
E4M3 = mybir.dt.float8_e4m3fn_x4
E5M2 = mybir.dt.float8_e5m2_x4
ALU = mybir.AluOpType

P = 128
J = 4
N = 512
STEPS = 16
LATE_FEATURES = 5


def tile_additivecoupling_pa_v_kernel(tc, x, h3, W4, b4, W5, b5, z4, grad_out, out_0, out_1):
    nc = tc.nc
    with ExitStack() as ctx:
        const = ctx.enter_context(tc.tile_pool(name="const", bufs=1))
        big = ctx.enter_context(tc.tile_pool(name="big", bufs=15))
        wide = ctx.enter_context(tc.tile_pool(name="wide", bufs=4))
        small = ctx.enter_context(tc.tile_pool(name="small", bufs=9))
        psum = ctx.enter_context(tc.psum_pool(name="psum", bufs=4))
        ctx.enter_context(tc.manual_schedule())

        ident = const.tile([P, P], F32, name="ident")
        make_identity(nc, ident[:])
        dz2_codes = const.tile([P, N], U32, name="dz2_codes", align_bytes=64)
        dz2_scales = const.tile([P, N], U8, name="dz2_scales", align_bytes=64)
        h3_codes = const.tile([P, MID], U32, name="h3_codes", align_bytes=64)
        h3_scales = const.tile([P, MID], U8, name="h3_scales", align_bytes=64)
        tok_codes = const.tile([P, MID], U32, name="tok_codes", align_bytes=64)
        tok_scales = const.tile([P, MID], U8, name="tok_scales", align_bytes=64)
        feat_codes = const.tile([P, J, 4, P], U32, name="feat_codes", align_bytes=64)
        feat_scales = const.tile([P, J, 4, P], U8, name="feat_scales", align_bytes=64)

        def copy(engine, out, in_):
            if engine == "S":
                nc.scalar.copy(out=out, in_=in_)
            else:
                nc.vector.tensor_copy(out=out, in_=in_)

        def load(shape, dtype, name, source):
            raw = big.tile(shape, dtype, tag="big", name=name, align_bytes=64)
            nc.sync.dma_start(out=raw[:], in_=source)
            return raw

        def quantize(grouped, codes, scales, fmt):
            nc.vector.quantize_mx(out=codes.bitcast(fmt), scales=scales, in_=grouped[:].rearrange("p c t -> p (c t)"))

        def turn(rows, engines, name):
            banks = []
            for pair in range(2):
                bank = psum.tile([P, 2, 2, P], F32, tag="turned", name="%s_bank_%d" % (name, pair))
                for i in range(2):
                    words = rows[2 * pair + i].bitcast(F32)
                    for u in range(2):
                        nc.tensor.transpose(bank[:, i, u, :], words[:, u::2], ident[:])
                banks.append(bank)
            grouped = small.tile([P, N, J], BF16, tag="grouped", name=name, align_bytes=64)
            out_words = grouped[:].rearrange("p c t -> p (c t)").bitcast(F32)
            for pair in range(2):
                half = out_words[:, N * pair : N * (pair + 1)].rearrange("p (i r u) -> p i r u", i=2, u=2)
                copy(engines[pair], half, banks[pair][:].rearrange("p i u r -> p i r u"))
            return grouped

        def interleave(engine, rows, name):
            grouped = small.tile([P, N, J], BF16, tag="grouped", name=name, align_bytes=64)
            copy(
                engine,
                grouped[:].rearrange("p (c i) t -> p c t i", i=4),
                rows.rearrange("p t (c i) -> p c t i", i=4),
            )
            return grouped

        z4_rows = z4.rearrange("(p j) o -> p j o", j=J)
        h3_rows = h3.rearrange("(p j) i -> p j i", j=J)
        raw_w5, raw_z4, raw_h3, raw_w4 = {}, {}, {}, {}

        def load_w5(half):
            rows = W5[2 * N * half : 2 * N * (half + 1), :].rearrange("(a p j) k -> p a j k", a=2, j=J)
            raw_w5[half] = load([P, 2, J, HALF], BF16, "raw_w5_%d" % half, rows)

        def load_z4(t):
            raw_z4[t] = load([P, MID], F32, "raw_z4_%d" % t, z4_rows[:, t, :])

        def load_h3(half):
            cols = slice(2 * N * half, 2 * N * (half + 1))
            raw_h3[half] = load([P, J, 2 * N], BF16, "raw_h3_%d" % half, h3_rows[:, :, cols])

        def load_w4(q, half):
            rows = W4[N * q : N * (q + 1), :].rearrange("(p j) o -> p j o", j=J)
            raw_w4[q, half] = load([P, 2, MID], BF16, "raw_w4_%d_%d" % (q, half), rows[:, 2 * half : 2 * half + 2, :])

        raw_grad = load([P, J, 2 * HALF], BF16, "raw_grad", grad_out.rearrange("(p j) d -> p j d", j=J))
        load_w5(0)
        load_w5(1)
        load_z4(0)
        load_z4(1)
        load_h3(0)
        load_z4(2)
        load_z4(3)
        load_w4(0, 0)
        load_w4(0, 1)
        load_h3(1)
        load_w4(1, 0)

        w5_codes = wide.tile([P, 4, N], U32, tag="wide", name="w5_codes", align_bytes=64)
        w5_scales = wide.tile([P, 4, N], U8, tag="scales", name="w5_scales", align_bytes=64)

        even = small.tile([P, J, HALF], BF16, tag="grouped", name="even", align_bytes=64)
        even_cols = raw_grad[:].rearrange("p j (k two) -> p j k two", two=2)[:, :, :, 0]
        nc.vector.tensor_copy(out=even[:, 0:2, :], in_=even_cols[:, 0:2, :])
        nc.scalar.copy(out=even[:, 2:J, :], in_=even_cols[:, 2:J, :])
        dz2_grouped = turn([even[:, j, :] for j in range(J)], "SS", "dz2_grouped")
        quantize(dz2_grouped, dz2_codes[:], dz2_scales[:], E5M2)

        def turn_w5(a):
            return turn([raw_w5[a // 2][:, a % 2, j, :] for j in range(J)], "SS", "w5_grouped_%d" % a)

        def quantize_w5(a, grouped):
            quantize(grouped, w5_codes[:, a, :], w5_scales[:, a, :], E4M3)

        w5_grouped = turn_w5(0)
        for a in range(1, 4):
            w5_next = turn_w5(a)
            quantize_w5(a - 1, w5_grouped)
            w5_grouped = w5_next
        quantize_w5(3, w5_grouped)

        dz1 = []
        for half in range(2):
            dz1_half = wide.tile([P, J, 2 * N], BF16, tag="wide", name="dz1_%d" % half, align_bytes=64)
            dz1.append(dz1_half)

        def dz1_chunk(a):
            return dz1[a // 2][:, :, N * (a % 2) : N * (a % 2 + 1)]

        def make_dz1(t):
            for a in range(4):
                dh = psum.tile([P, N], F32, tag="sums", name="dh_%d_%d" % (t, a))
                nc.tensor.matmul_mx(
                    out=dh[:],
                    lhsT=dz2_codes[:, P * t : P * (t + 1)].bitcast(E5M2),
                    lhsT_scale=dz2_scales[:, P * t : P * (t + 1)],
                    rhs=w5_codes[:, a, :].bitcast(E4M3),
                    rhs_scale=w5_scales[:, a, :],
                    start=True,
                    stop=True,
                )
                nc.vector.scalar_tensor_tensor(
                    out=dz1_chunk(a)[:, t, :].rearrange("p (m j) -> p m j", j=J),
                    in0=raw_z4[t][:, N * a : N * (a + 1)].rearrange("p (m j) -> p m j", j=J),
                    scalar=0.0,
                    in1=dh[:].rearrange("p (j m) -> p m j", j=J),
                    op0=ALU.is_gt,
                    op1=ALU.mult,
                )

        def turn_dz1(t):
            return turn([dz1_chunk(g)[:, t, :] for g in range(4)], "SS", "feat_grouped_%d" % t)

        def quantize_feat(t, grouped):
            codes = feat_codes[:, t, :, :].rearrange("p g r -> p (g r)")
            scales = feat_scales[:, t, :, :].rearrange("p g r -> p (g r)")
            quantize(grouped, codes, scales, E5M2)

        def interleave_tok(engine, a):
            return interleave(engine, dz1_chunk(a), "tok_grouped_%d" % a)

        def quantize_tok(a, grouped):
            cols = slice(N * a, N * (a + 1))
            quantize(grouped, tok_codes[:, cols], tok_scales[:, cols], E5M2)

        def interleave_h3(engine, a):
            return interleave(engine, raw_h3[a // 2][:, :, N * (a % 2) : N * (a % 2 + 1)], "h3_grouped_%d" % a)

        def quantize_h3(a, grouped):
            cols = slice(N * a, N * (a + 1))
            quantize(grouped, h3_codes[:, cols], h3_scales[:, cols], E4M3)

        feat_grouped = {}
        make_dz1(0)
        make_dz1(1)
        load_w4(1, 1)
        h3_grouped = interleave_h3("S", 0)
        feat_grouped[0] = turn_dz1(0)
        make_dz1(2)
        feat_grouped[1] = turn_dz1(1)
        make_dz1(3)
        tok_grouped = {0: interleave_tok("S", 0)}
        load_w4(2, 0)
        load_w4(2, 1)
        quantize_h3(0, h3_grouped)
        feat_grouped[2] = turn_dz1(2)
        tok_grouped[1] = interleave_tok("V", 1)
        quantize_tok(0, tok_grouped[0])
        tok_grouped[3] = interleave_tok("S", 3)
        tok_grouped[2] = interleave_tok("V", 2)
        quantize_tok(1, tok_grouped[1])
        quantize_tok(2, tok_grouped[2])
        feat_grouped[3] = turn_dz1(3)
        quantize_tok(3, tok_grouped[3])

        w4_codes, w4_scales = {}, {}

        def turn_w4(unit):
            q, g = divmod(unit, 4)
            if g == 0:
                w4_codes[q] = wide.tile([P, 4, N], U32, tag="wide", name="w4_codes_%d" % q, align_bytes=64)
                w4_scales[q] = wide.tile([P, 4, N], U8, tag="scales", name="w4_scales_%d" % q, align_bytes=64)
            rows = [raw_w4[q, j // 2][:, j % 2, N * g : N * (g + 1)] for j in range(J)]
            return turn(rows, "SS", "w4_grouped_%d" % unit)

        def quantize_w4(unit, grouped):
            q, g = divmod(unit, 4)
            quantize(grouped, w4_codes[q][:, g, :], w4_scales[q][:, g, :], E4M3)

        def out_1_tile(s):
            rows = slice(P * s, P * (s + 1))
            result = big.tile([P, MID], F32, tag="big", name="out_1_rows_%d" % s, align_bytes=64)
            for a in range(4):
                cols = slice(N * a, N * (a + 1))
                acc = psum.tile([P, N], F32, tag="sums", name="out_1_%d_%d" % (s, a))
                nc.tensor.matmul_mx(
                    out=acc[:],
                    lhsT=h3_codes[:, rows].bitcast(E4M3),
                    lhsT_scale=h3_scales[:, rows],
                    rhs=tok_codes[:, cols].bitcast(E5M2),
                    rhs_scale=tok_scales[:, cols],
                    start=True,
                    stop=True,
                )
                copy("VS"[a % 2], result[:, cols], acc[:])
            nc.sync.dma_start(out=out_1[rows, :], in_=result[:])

        for s in range(STEPS):
            w4_next = turn_w4(s)
            chunk = s // 4 + 1
            h3_due = s % 4 == 1 and chunk < 4
            if h3_due:
                h3_grouped = interleave_h3("V", chunk)
            if s > 0:
                quantize_w4(s - 1, w4_grouped)
            w4_grouped = w4_next
            if LATE_FEATURES <= s < LATE_FEATURES + J:
                quantize_feat(s - LATE_FEATURES, feat_grouped[s - LATE_FEATURES])
            out_1_tile(s)
            if s < 2:
                load_w4(3, s)
            if h3_due:
                quantize_h3(chunk, h3_grouped)
        quantize_w4(STEPS - 1, w4_grouped)

        out_0_rows = out_0.rearrange("(p j) i -> p j i", j=J)
        for t in range(J):
            result = big.tile([P, MID], F32, tag="big", name="out_0_rows_%d" % t, align_bytes=64)
            for q in range(4):
                acc = psum.tile([P, N], F32, tag="sums", name="out_0_%d_%d" % (t, q))
                for g in range(4):
                    nc.tensor.matmul_mx(
                        out=acc[:],
                        lhsT=feat_codes[:, t, g, :].bitcast(E5M2),
                        lhsT_scale=feat_scales[:, t, g, :],
                        rhs=w4_codes[q][:, g, :].bitcast(E4M3),
                        rhs_scale=w4_scales[q][:, g, :],
                        start=(g == 0),
                        stop=(g == 3),
                    )
                cols = slice(N * q, N * (q + 1))
                copy("SV"[q % 2], result[:, cols].rearrange("p (m j) -> p m j", j=J), acc[:].rearrange("p (j m) -> p m j", j=J))
                if t == J - 1 and q >= 1:
                    ready = slice(0 if q == 1 else N * q, N * (q + 1))
                    nc.sync.dma_start(out=out_0_rows[:, t, ready], in_=result[:, ready])
            if t < J - 1:
                nc.sync.dma_start(out=out_0_rows[:, t, :], in_=result[:])
